import numpy as np
import ml_dtypes


def mxq(x, axis, fmt="e4m3"):
    dtype, down = {"e4m3": (ml_dtypes.float8_e4m3fn, 7), "e5m2": (ml_dtypes.float8_e5m2, 14)}[fmt]
    v = np.moveaxis(np.asarray(x, np.float32).astype(ml_dtypes.bfloat16).astype(np.float64), axis, -1)
    blocks = v.reshape(v.shape[:-1] + (-1, 32))
    amax = np.abs(blocks).max(-1, keepdims=True)
    byte = np.maximum(np.where(amax > 0, np.frexp(amax)[1] - 1 + 127, 0) - down, 1)
    scale = np.exp2(byte - 127.0)
    codes = (blocks / scale).astype(np.float32).astype(dtype).astype(np.float64)
    return np.moveaxis((codes * scale).reshape(v.shape), -1, axis)


WIDE = False


def mx_kscale(k):
    if not WIDE:
        return np.ones(k)
    levels = np.array([10, -10, 5, -5, 0])
    a = np.random.permutation(np.resize(levels, k // 512 * 4)).reshape(k // 512, 4)
    idx = np.arange(k)
    return np.exp2(a[idx // 512, idx % 128 // 32])


BF16 = ml_dtypes.bfloat16


def bf(x):
    return np.asarray(x, np.float32).astype(BF16)


def f64(x):
    return np.asarray(x).astype(np.float64)


B, S, H, NH, FF = 2, 512, 1024, 8, 3072
EPS = 1e-7


def layer_norm(x, g, b):
    m = x.mean(-1, keepdims=True)
    v = ((x - m) ** 2).mean(-1, keepdims=True)
    return (x - m) / np.sqrt(v + EPS) * g + b


def setup_inputs():
    s = mx_kscale(FF)
    r = np.random.standard_normal
    return {"ff": bf(r((B, S, FF)) * 0.65 * s), "attn_out": bf(r((B, S, H))),
            "Wf": bf(r((FF, H)) * 1.5 / np.sqrt(FF) / s[:, None]), "b_f": bf(r(H) * 0.2),
            "ln2_g": bf(1.0 + 0.1 * r(H)), "ln2_b": bf(0.1 * r(H))}


def reference(ff, attn_out, Wf, b_f, ln2_g, ln2_b):
    u = (mxq(f64(ff), 2, "e4m3") @ mxq(f64(Wf), 0, "e4m3")) + f64(b_f) + f64(attn_out)
    return layer_norm(u, f64(ln2_g), f64(ln2_b))

@@ -1,0 +1,275 @@
+from contextlib import ExitStack
+
+import concourse.mybir as mybir
+from concourse.masks import make_identity
+
+F32 = mybir.dt.float32
+BF16 = mybir.dt.bfloat16
+U32 = mybir.dt.uint32
+U8 = mybir.dt.uint8
+FP8X4 = mybir.dt.float8_e4m3fn_x4
+ALU = mybir.AluOpType
+ACT = mybir.ActivationFunctionType
+
+P = 128
+PACK = 4
+K_PASS = P * PACK
+TOKENS = 1024
+K = 3072
+N = 1024
+EPS = 1e-7
+PASSES = K // K_PASS
+TILES = TOKENS // P
+BANK = 512
+HALVES = N // BANK
+FILLS = K // 2 // BANK
+PASSES_PER_FILL = PASSES // FILLS
+
+EARLY_TILES = 2
+STAGE_BANKS = 8 - EARLY_TILES * HALVES
+W_VECTOR_COLS = 512
+
+FLOPS = 2 * TOKENS * K * N
+
+
+def tile_disentangledattention_pc_kernel(tc, ff, attn_out, Wf, b_f, ln2_g, ln2_b, out):
+    nc = tc.nc
+    ff_rows = ff.flatten_outer_dims()
+    attn_rows = attn_out.flatten_outer_dims()
+    out_rows = out.flatten_outer_dims()
+
+    with ExitStack() as ctx:
+        const = ctx.enter_context(tc.tile_pool(name="const", bufs=1))
+        ff_pool = ctx.enter_context(tc.tile_pool(name="ff", bufs=TILES))
+        attn_pool = ctx.enter_context(tc.tile_pool(name="attn", bufs=TILES))
+        w_raw_pool = ctx.enter_context(tc.tile_pool(name="w_raw", bufs=4))
+        w_grouped_pool = ctx.enter_context(tc.tile_pool(name="w_grouped", bufs=2))
+        x_grouped_pool = ctx.enter_context(tc.tile_pool(name="x_grouped", bufs=2))
+        x_pool = ctx.enter_context(tc.tile_pool(name="x", bufs=EARLY_TILES + 2))
+        resid_pool = ctx.enter_context(tc.tile_pool(name="resid", bufs=3))
+        u_pool = ctx.enter_context(tc.tile_pool(name="u", bufs=2))
+        y_pool = ctx.enter_context(tc.tile_pool(name="y", bufs=3))
+        scratch = ctx.enter_context(tc.tile_pool(name="scratch", bufs=2))
+        stats = ctx.enter_context(tc.tile_pool(name="stats", bufs=4))
+        acc_pool = ctx.enter_context(tc.psum_pool(name="acc", bufs=EARLY_TILES * HALVES))
+        stage = ctx.enter_context(tc.psum_pool(name="stage", bufs=STAGE_BANKS))
+        ctx.enter_context(tc.manual_schedule())
+
+        ident_words = const.tile([P, P], F32)
+        make_identity(nc, ident_words[:])
+        ident_bf16 = const.tile([P, P], BF16)
+        make_identity(nc, ident_bf16[:])
+        vector_rows = const.tile([P, N], BF16)
+        nc.vector.memset(vector_rows[:], 0.0)
+        pick = const.tile([P, 3, P], BF16)
+        nc.vector.memset(pick[:], 0.0)
+        for j, vec in enumerate((b_f, ln2_g, ln2_b)):
+            nc.sync.dma_start(out=vector_rows[32 * j : 32 * j + 1, :], in_=vec.rearrange("(o n) -> o n", o=1))
+            nc.vector.memset(pick[32 * j : 32 * j + 1, j, :], 1.0)
+        eps = const.tile([P, 1], F32)
+        nc.vector.memset(eps[:], EPS)
+        warm = const.tile([P, 1], F32)
+        nc.scalar.activation(out=warm[:], in_=eps[:], func=ACT.Sqrt)
+        gamma = const.tile([P, N], F32)
+        beta = const.tile([P, N], F32)
+
+        def spread_gain_and_shift():
+            for h in range(HALVES):
+                cols = slice(h * BANK, (h + 1) * BANK)
+                gamma_bank = stage.tile([P, BANK], F32, name="bank")
+                nc.tensor.matmul(out=gamma_bank[:], lhsT=pick[:, 1, :], rhs=vector_rows[:, cols], start=True, stop=True)
+                nc.vector.tensor_copy(out=gamma[:, cols], in_=gamma_bank[:])
+                beta_bank = stage.tile([P, BANK], F32, name="bank")
+                nc.tensor.matmul(out=beta_bank[:], lhsT=pick[:, 2, :], rhs=vector_rows[:, cols], start=True, stop=True)
+                nc.scalar.copy(out=beta[:, cols], in_=beta_bank[:])
+
+        w_codes = const.tile([P, PASSES, N], U32, align_bytes=64)
+        w_scales = const.tile([P, PASSES, N], U8, align_bytes=64)
+
+        ff_tile, attn_tile, w_raw, w_grouped = {}, {}, {}, {}
+        x_grouped, x_codes, x_scales = {}, {}, {}
+        acc, resid, u, y, neg_mean, std = {}, {}, {}, {}, {}, {}
+
+        def load_tokens(m):
+            ff_tile[m] = ff_pool.tile([P, K], BF16, name="ff_tile")
+            nc.sync.dma_start(out=ff_tile[m][:], in_=ff_rows[m * P : (m + 1) * P, :])
+
+        def load_residual(m):
+            attn_tile[m] = attn_pool.tile([P, N], BF16, name="attn_tile")
+            nc.sync.dma_start(out=attn_tile[m][:], in_=attn_rows[m * P : (m + 1) * P, :])
+
+        def load_weights(g):
+            w_raw[g] = w_raw_pool.tile([P, PACK, N], BF16, name="w_raw")
+            nc.sync.dma_start(
+                out=w_raw[g][:].rearrange("p (u e) c -> p u (e c)", u=2),
+                in_=Wf[g * K_PASS : (g + 1) * K_PASS, :].rearrange("(u p e) c -> p u (e c)", u=2, e=2),
+            )
+
+        def regroup_weights(g):
+            w_grouped[g] = w_grouped_pool.tile([P, N, PACK], BF16, name="w_grouped", align_bytes=64)
+            left = slice(0, W_VECTOR_COLS)
+            right = slice(W_VECTOR_COLS, N)
+            nc.vector.tensor_copy(
+                out=w_grouped[g][:, left, :].rearrange("p (c i) t -> p c t i", i=4),
+                in_=w_raw[g][:, :, left].rearrange("p t (c i) -> p c t i", i=4),
+            )
+            nc.scalar.copy(
+                out=w_grouped[g][:, right, :].rearrange("p (c i) t -> p c t i", i=4),
+                in_=w_raw[g][:, :, right].rearrange("p t (c i) -> p c t i", i=4),
+            )
+
+        def quantise_weights(g):
+            for h in range(HALVES):
+                cols = slice(h * BANK, (h + 1) * BANK)
+                nc.vector.quantize_mx(
+                    out=w_codes[:, g, cols].bitcast(FP8X4),
+                    scales=w_scales[:, g, cols],
+                    in_=w_grouped[g][:, cols, :].rearrange("p c t -> p (c t)"),
+                )
+
+        def transpose_tokens(m, j):
+            if j == 0:
+                x_grouped[m] = x_grouped_pool.tile([P, PASSES * P * PACK], BF16, name="x_grouped", align_bytes=64)
+            words = ff_tile[m][:].bitcast(F32)
+            bank = stage.tile([P, BANK], F32, name="bank")
+            for q in range(BANK // P):
+                first = j * BANK + q * P
+                nc.tensor.transpose(bank[:, q * P : (q + 1) * P], words[:, first : first + P], ident_words[:])
+            nc.scalar.copy(
+                out=x_grouped[m][:].bitcast(F32)[:, j * BANK : (j + 1) * BANK].rearrange(
+                    "p (g r u) -> p g r u", g=PASSES_PER_FILL, u=2
+                ),
+                in_=bank[:].rearrange("p (g u r) -> p g r u", g=PASSES_PER_FILL, u=2),
+            )
+
+        def quantise_tokens(m):
+            x_codes[m] = x_pool.tile([P, PASSES * P], U32, name="x_codes", align_bytes=64)
+            x_scales[m] = x_pool.tile([P, PASSES * P], U8, name="x_scales", align_bytes=64)
+            width = PASSES_PER_FILL * P
+            for j in range(FILLS):
+                nc.vector.quantize_mx(
+                    out=x_codes[m][:, j * width : (j + 1) * width].bitcast(FP8X4),
+                    scales=x_scales[m][:, j * width : (j + 1) * width],
+                    in_=x_grouped[m][:, j * width * PACK : (j + 1) * width * PACK],
+                )
+
+        def multiply(m, g):
+            if g == 0:
+                acc[m] = [acc_pool.tile([P, BANK], F32, name="acc") for h in range(HALVES)]
+            tokens = slice(g * P, (g + 1) * P)
+            for h in range(HALVES):
+                cols = slice(h * BANK, (h + 1) * BANK)
+                nc.tensor.matmul_mx(
+                    out=acc[m][h][:],
+                    lhsT=x_codes[m][:, tokens].bitcast(FP8X4),
+                    lhsT_scale=x_scales[m][:, tokens],
+                    rhs=w_codes[:, g, cols].bitcast(FP8X4),
+                    rhs_scale=w_scales[:, g, cols],
+                    start=(g == 0),
+                    stop=(g == PASSES - 1),
+                )
+
+        def add_residual_and_bias(m):
+            resid[m] = resid_pool.tile([P, N], F32, name="resid")
+            for h in range(HALVES):
+                cols = slice(h * BANK, (h + 1) * BANK)
+                bank = stage.tile([P, BANK], F32, name="bank")
+                nc.tensor.matmul(out=bank[:], lhsT=ident_bf16[:], rhs=attn_tile[m][:, cols], start=True, stop=False)
+                nc.tensor.matmul(out=bank[:], lhsT=pick[:, 0, :], rhs=vector_rows[:, cols], start=False, stop=True)
+                nc.scalar.copy(out=resid[m][:, cols], in_=bank[:])
+
+        def form_u(m):
+            u[m] = u_pool.tile([P, N], F32, name="u")
+            half_sums = stats.tile([P, HALVES], F32, name="half_sums")
+            for h in range(HALVES):
+                cols = slice(h * BANK, (h + 1) * BANK)
+                nc.vector.scalar_tensor_tensor(
+                    out=u[m][:, cols],
+                    in0=acc[m][h][:],
+                    scalar=1.0,
+                    in1=resid[m][:, cols],
+                    op0=ALU.mult,
+                    op1=ALU.add,
+                    accum_out=half_sums[:, h : h + 1],
+                )
+            neg_mean[m] = stats.tile([P, 1], F32, name="neg_mean")
+            nc.vector.tensor_scalar(
+                out=neg_mean[m][:],
+                in0=half_sums[:, 0:1],
+                scalar1=half_sums[:, 1:2],
+                scalar2=-1.0 / N,
+                op0=ALU.add,
+                op1=ALU.mult,
+            )
+
+        def deviation(m):
+            squares = scratch.tile([P, N], BF16, name="squares")
+            sum_squares = stats.tile([P, 1], F32, name="sum_squares")
+            nc.scalar.activation(
+                out=squares[:], in_=u[m][:], func=ACT.Square, bias=neg_mean[m][:], scale=1.0, accum_out=sum_squares[:]
+            )
+            std[m] = stats.tile([P, 1], F32, name="std")
+            nc.scalar.activation(out=std[m][:], in_=sum_squares[:], func=ACT.Sqrt, bias=eps[:], scale=1.0 / N)
+
+        def centre_and_gain(m):
+            y[m] = y_pool.tile([P, N], F32, name="y")
+            nc.vector.scalar_tensor_tensor(
+                out=y[m][:], in0=u[m][:], scalar=neg_mean[m][:], in1=gamma[:], op0=ALU.add, op1=ALU.mult
+            )
+
+        def scale_shift_store(m):
+            rstd = stats.tile([P, 1], F32, name="rstd")
+            nc.vector.reciprocal(out=rstd[:], in_=std[m][:])
+            nc.vector.scalar_tensor_tensor(
+                out=y[m][:], in0=y[m][:], scalar=rstd[:], in1=beta[:], op0=ALU.mult, op1=ALU.add
+            )
+            nc.sync.dma_start(out=out_rows[m * P : (m + 1) * P, :], in_=y[m][:])
+
+        for step in range(PASSES):
+            load_weights(step)
+            if step < EARLY_TILES:
+                load_tokens(step)
+            if step == 0:
+                spread_gain_and_shift()
+            regroup_weights(step)
+            if 1 <= step <= EARLY_TILES:
+                quantise_tokens(step - 1)
+            quantise_weights(step)
+            if step < EARLY_TILES:
+                for j in range(FILLS):
+                    transpose_tokens(step, j)
+            if step == PASSES - 1:
+                load_residual(0)
+                add_residual_and_bias(0)
+            for m in range(EARLY_TILES):
+                for g in range(PASSES):
+                    if max(m + 1, g) == step:
+                        multiply(m, g)
+
+        for m in range(EARLY_TILES, TILES):
+            load_tokens(m)
+            load_residual(m - EARLY_TILES + 1)
+        for m in range(TILES - EARLY_TILES + 1, TILES):
+            load_residual(m)
+        for j in range(FILLS):
+            transpose_tokens(EARLY_TILES, j)
+
+        for s in range(TILES):
+            multiplied = s + EARLY_TILES
+            transposed = multiplied + 1
+            if s + 1 < TILES:
+                add_residual_and_bias(s + 1)
+            form_u(s)
+            deviation(s)
+            if s >= 1:
+                scale_shift_store(s - 1)
+            centre_and_gain(s)
+            if multiplied < TILES:
+                quantise_tokens(multiplied)
+            if transposed < TILES:
+                for j in range(FILLS):
+                    transpose_tokens(transposed, j)
+            if multiplied < TILES:
+                for g in range(PASSES):
+                    multiply(multiplied, g)
+        scale_shift_store(TILES - 1)

@@ -26,7 +26,7 @@ FILLS = K // 2 // BANK
 PASSES_PER_FILL = PASSES // FILLS
 
 EARLY_TILES = 2
-STAGE_BANKS = 8 - EARLY_TILES * HALVES
+STAGE_BANKS = 2
 W_VECTOR_COLS = 512
 
 FLOPS = 2 * TOKENS * K * N
@@ -53,12 +53,11 @@ def tile_disentangledattention_pc_kernel(tc, ff, attn_out, Wf, b_f, ln2_g, ln2_b
         stats = ctx.enter_context(tc.tile_pool(name="stats", bufs=4))
         acc_pool = ctx.enter_context(tc.psum_pool(name="acc", bufs=EARLY_TILES * HALVES))
         stage = ctx.enter_context(tc.psum_pool(name="stage", bufs=STAGE_BANKS))
+        norm_pool = ctx.enter_context(tc.psum_pool(name="norm", bufs=1))
         ctx.enter_context(tc.manual_schedule())
 
         ident_words = const.tile([P, P], F32)
         make_identity(nc, ident_words[:])
-        ident_bf16 = const.tile([P, P], BF16)
-        make_identity(nc, ident_bf16[:])
         vector_rows = const.tile([P, N], BF16)
         nc.vector.memset(vector_rows[:], 0.0)
         pick = const.tile([P, 3, P], BF16)
@@ -70,18 +69,18 @@ def tile_disentangledattention_pc_kernel(tc, ff, attn_out, Wf, b_f, ln2_g, ln2_b
         nc.vector.memset(eps[:], EPS)
         warm = const.tile([P, 1], F32)
         nc.scalar.activation(out=warm[:], in_=eps[:], func=ACT.Sqrt)
-        gamma = const.tile([P, N], F32)
-        beta = const.tile([P, N], F32)
+        gamma = norm_pool.tile([P, N], BF16)
+        beta = norm_pool.tile([P, N], BF16)
+        bias = const.tile([P, N], BF16)
 
-        def spread_gain_and_shift():
+        def spread_vectors():
             for h in range(HALVES):
                 cols = slice(h * BANK, (h + 1) * BANK)
-                gamma_bank = stage.tile([P, BANK], F32, name="bank")
-                nc.tensor.matmul(out=gamma_bank[:], lhsT=pick[:, 1, :], rhs=vector_rows[:, cols], start=True, stop=True)
-                nc.vector.tensor_copy(out=gamma[:, cols], in_=gamma_bank[:])
-                beta_bank = stage.tile([P, BANK], F32, name="bank")
-                nc.tensor.matmul(out=beta_bank[:], lhsT=pick[:, 2, :], rhs=vector_rows[:, cols], start=True, stop=True)
-                nc.scalar.copy(out=beta[:, cols], in_=beta_bank[:])
+                bank = stage.tile([P, BANK], F32, name="bank")
+                nc.tensor.matmul(out=bank[:], lhsT=pick[:, 0, :], rhs=vector_rows[:, cols], start=True, stop=True)
+                nc.scalar.copy(out=bias[:, cols], in_=bank[:])
+                nc.tensor.matmul(out=gamma[:, cols], lhsT=pick[:, 1, :], rhs=vector_rows[:, cols], start=True, stop=True)
+                nc.tensor.matmul(out=beta[:, cols], lhsT=pick[:, 2, :], rhs=vector_rows[:, cols], start=True, stop=True)
 
         w_codes = const.tile([P, PASSES, N], U32, align_bytes=64)
         w_scales = const.tile([P, PASSES, N], U8, align_bytes=64)
@@ -171,12 +170,7 @@ def tile_disentangledattention_pc_kernel(tc, ff, attn_out, Wf, b_f, ln2_g, ln2_b
 
         def add_residual_and_bias(m):
             resid[m] = resid_pool.tile([P, N], F32, name="resid")
-            for h in range(HALVES):
-                cols = slice(h * BANK, (h + 1) * BANK)
-                bank = stage.tile([P, BANK], F32, name="bank")
-                nc.tensor.matmul(out=bank[:], lhsT=ident_bf16[:], rhs=attn_tile[m][:, cols], start=True, stop=False)
-                nc.tensor.matmul(out=bank[:], lhsT=pick[:, 0, :], rhs=vector_rows[:, cols], start=False, stop=True)
-                nc.scalar.copy(out=resid[m][:, cols], in_=bank[:])
+            nc.gpsimd.tensor_tensor(out=resid[m][:], in0=attn_tile[m][:], in1=bias[:], op=ALU.add)
 
         def form_u(m):
             u[m] = u_pool.tile([P, N], F32, name="u")
@@ -225,12 +219,14 @@ def tile_disentangledattention_pc_kernel(tc, ff, attn_out, Wf, b_f, ln2_g, ln2_b
             )
             nc.sync.dma_start(out=out_rows[m * P : (m + 1) * P, :], in_=y[m][:])
 
+        load_residual(0)
         for step in range(PASSES):
             load_weights(step)
             if step < EARLY_TILES:
                 load_tokens(step)
             if step == 0:
-                spread_gain_and_shift()
+                spread_vectors()
+                add_residual_and_bias(0)
             regroup_weights(step)
             if 1 <= step <= EARLY_TILES:
                 quantise_tokens(step - 1)
@@ -238,17 +234,14 @@ def tile_disentangledattention_pc_kernel(tc, ff, attn_out, Wf, b_f, ln2_g, ln2_b
             if step < EARLY_TILES:
                 for j in range(FILLS):
                     transpose_tokens(step, j)
-            if step == PASSES - 1:
-                load_residual(0)
-                add_residual_and_bias(0)
             for m in range(EARLY_TILES):
                 for g in range(PASSES):
                     if max(m + 1, g) == step:
                         multiply(m, g)
 
         for m in range(EARLY_TILES, TILES):
-            load_tokens(m)
             load_residual(m - EARLY_TILES + 1)
+            load_tokens(m)
         for m in range(TILES - EARLY_TILES + 1, TILES):
             load_residual(m)
         for j in range(FILLS):
@@ -267,9 +260,15 @@ def tile_disentangledattention_pc_kernel(tc, ff, attn_out, Wf, b_f, ln2_g, ln2_b
             if multiplied < TILES:
                 quantise_tokens(multiplied)
             if transposed < TILES:
-                for j in range(FILLS):
+                for j in range(STAGE_BANKS):
                     transpose_tokens(transposed, j)
             if multiplied < TILES:
-                for g in range(PASSES):
+                for g in range(PASSES // 2):
+                    multiply(multiplied, g)
+            if transposed < TILES:
+                for j in range(STAGE_BANKS, FILLS):
+                    transpose_tokens(transposed, j)
+            if multiplied < TILES:
+                for g in range(PASSES // 2, PASSES):
                     multiply(multiplied, g)
         scale_shift_store(TILES - 1)

@@ -26,7 +26,7 @@ FILLS = K // 2 // BANK
 PASSES_PER_FILL = PASSES // FILLS
 
 EARLY_TILES = 2
-STAGE_BANKS = 2
+STAGE_BANKS = 8 - EARLY_TILES * HALVES
 W_VECTOR_COLS = 512
 
 FLOPS = 2 * TOKENS * K * N
@@ -53,11 +53,11 @@ def tile_disentangledattention_pc_kernel(tc, ff, attn_out, Wf, b_f, ln2_g, ln2_b
         stats = ctx.enter_context(tc.tile_pool(name="stats", bufs=4))
         acc_pool = ctx.enter_context(tc.psum_pool(name="acc", bufs=EARLY_TILES * HALVES))
         stage = ctx.enter_context(tc.psum_pool(name="stage", bufs=STAGE_BANKS))
-        norm_pool = ctx.enter_context(tc.psum_pool(name="norm", bufs=1))
-        ctx.enter_context(tc.manual_schedule())
 
         ident_words = const.tile([P, P], F32)
         make_identity(nc, ident_words[:])
+        ident_bf16 = const.tile([P, P], BF16)
+        make_identity(nc, ident_bf16[:])
         vector_rows = const.tile([P, N], BF16)
         nc.vector.memset(vector_rows[:], 0.0)
         pick = const.tile([P, 3, P], BF16)
@@ -69,18 +69,18 @@ def tile_disentangledattention_pc_kernel(tc, ff, attn_out, Wf, b_f, ln2_g, ln2_b
         nc.vector.memset(eps[:], EPS)
         warm = const.tile([P, 1], F32)
         nc.scalar.activation(out=warm[:], in_=eps[:], func=ACT.Sqrt)
-        gamma = norm_pool.tile([P, N], BF16)
-        beta = norm_pool.tile([P, N], BF16)
-        bias = const.tile([P, N], BF16)
+        gamma = const.tile([P, N], F32)
+        beta = const.tile([P, N], F32)
 
-        def spread_vectors():
+        def spread_gain_and_shift():
             for h in range(HALVES):
                 cols = slice(h * BANK, (h + 1) * BANK)
-                bank = stage.tile([P, BANK], F32, name="bank")
-                nc.tensor.matmul(out=bank[:], lhsT=pick[:, 0, :], rhs=vector_rows[:, cols], start=True, stop=True)
-                nc.scalar.copy(out=bias[:, cols], in_=bank[:])
-                nc.tensor.matmul(out=gamma[:, cols], lhsT=pick[:, 1, :], rhs=vector_rows[:, cols], start=True, stop=True)
-                nc.tensor.matmul(out=beta[:, cols], lhsT=pick[:, 2, :], rhs=vector_rows[:, cols], start=True, stop=True)
+                gamma_bank = stage.tile([P, BANK], F32, name="bank")
+                nc.tensor.matmul(out=gamma_bank[:], lhsT=pick[:, 1, :], rhs=vector_rows[:, cols], start=True, stop=True)
+                nc.vector.tensor_copy(out=gamma[:, cols], in_=gamma_bank[:])
+                beta_bank = stage.tile([P, BANK], F32, name="bank")
+                nc.tensor.matmul(out=beta_bank[:], lhsT=pick[:, 2, :], rhs=vector_rows[:, cols], start=True, stop=True)
+                nc.scalar.copy(out=beta[:, cols], in_=beta_bank[:])
 
         w_codes = const.tile([P, PASSES, N], U32, align_bytes=64)
         w_scales = const.tile([P, PASSES, N], U8, align_bytes=64)
@@ -170,7 +170,12 @@ def tile_disentangledattention_pc_kernel(tc, ff, attn_out, Wf, b_f, ln2_g, ln2_b
 
         def add_residual_and_bias(m):
             resid[m] = resid_pool.tile([P, N], F32, name="resid")
-            nc.gpsimd.tensor_tensor(out=resid[m][:], in0=attn_tile[m][:], in1=bias[:], op=ALU.add)
+            for h in range(HALVES):
+                cols = slice(h * BANK, (h + 1) * BANK)
+                bank = stage.tile([P, BANK], F32, name="bank")
+                nc.tensor.matmul(out=bank[:], lhsT=ident_bf16[:], rhs=attn_tile[m][:, cols], start=True, stop=False)
+                nc.tensor.matmul(out=bank[:], lhsT=pick[:, 0, :], rhs=vector_rows[:, cols], start=False, stop=True)
+                nc.scalar.copy(out=resid[m][:, cols], in_=bank[:])
 
         def form_u(m):
             u[m] = u_pool.tile([P, N], F32, name="u")
@@ -219,14 +224,12 @@ def tile_disentangledattention_pc_kernel(tc, ff, attn_out, Wf, b_f, ln2_g, ln2_b
             )
             nc.sync.dma_start(out=out_rows[m * P : (m + 1) * P, :], in_=y[m][:])
 
-        load_residual(0)
         for step in range(PASSES):
             load_weights(step)
             if step < EARLY_TILES:
                 load_tokens(step)
             if step == 0:
-                spread_vectors()
-                add_residual_and_bias(0)
+                spread_gain_and_shift()
             regroup_weights(step)
             if 1 <= step <= EARLY_TILES:
                 quantise_tokens(step - 1)
@@ -234,14 +237,17 @@ def tile_disentangledattention_pc_kernel(tc, ff, attn_out, Wf, b_f, ln2_g, ln2_b
             if step < EARLY_TILES:
                 for j in range(FILLS):
                     transpose_tokens(step, j)
+            if step == PASSES - 1:
+                load_residual(0)
+                add_residual_and_bias(0)
             for m in range(EARLY_TILES):
                 for g in range(PASSES):
                     if max(m + 1, g) == step:
                         multiply(m, g)
 
         for m in range(EARLY_TILES, TILES):
-            load_residual(m - EARLY_TILES + 1)
             load_tokens(m)
+            load_residual(m - EARLY_TILES + 1)
         for m in range(TILES - EARLY_TILES + 1, TILES):
             load_residual(m)
         for j in range(FILLS):
@@ -260,15 +266,9 @@ def tile_disentangledattention_pc_kernel(tc, ff, attn_out, Wf, b_f, ln2_g, ln2_b
             if multiplied < TILES:
                 quantise_tokens(multiplied)
             if transposed < TILES:
-                for j in range(STAGE_BANKS):
+                for j in range(FILLS):
                     transpose_tokens(transposed, j)
             if multiplied < TILES:
-                for g in range(PASSES // 2):
-                    multiply(multiplied, g)
-            if transposed < TILES:
-                for j in range(STAGE_BANKS, FILLS):
-                    transpose_tokens(transposed, j)
-            if multiplied < TILES:
-                for g in range(PASSES // 2, PASSES):
+                for g in range(PASSES):
                     multiply(multiplied, g)
         scale_shift_store(TILES - 1)

from contextlib import ExitStack

import concourse.mybir as mybir
from concourse.masks import make_identity

F32 = mybir.dt.float32
BF16 = mybir.dt.bfloat16
U32 = mybir.dt.uint32
U8 = mybir.dt.uint8
FP8X4 = mybir.dt.float8_e4m3fn_x4
ALU = mybir.AluOpType
ACT = mybir.ActivationFunctionType

P = 128
PACK = 4
K_PASS = P * PACK
TOKENS = 1024
K = 3072
N = 1024
EPS = 1e-7
PASSES = K // K_PASS
TILES = TOKENS // P
BANK = 512
HALVES = N // BANK
FILLS = K // 2 // BANK
PASSES_PER_FILL = PASSES // FILLS

EARLY_TILES = 2
STAGE_BANKS = 8 - EARLY_TILES * HALVES
W_VECTOR_COLS = 512

FLOPS = 2 * TOKENS * K * N


def tile_disentangledattention_pc_kernel(tc, ff, attn_out, Wf, b_f, ln2_g, ln2_b, out):
    nc = tc.nc
    ff_rows = ff.flatten_outer_dims()
    attn_rows = attn_out.flatten_outer_dims()
    out_rows = out.flatten_outer_dims()

    with ExitStack() as ctx:
        const = ctx.enter_context(tc.tile_pool(name="const", bufs=1))
        ff_pool = ctx.enter_context(tc.tile_pool(name="ff", bufs=TILES))
        attn_pool = ctx.enter_context(tc.tile_pool(name="attn", bufs=TILES))
        w_raw_pool = ctx.enter_context(tc.tile_pool(name="w_raw", bufs=4))
        w_grouped_pool = ctx.enter_context(tc.tile_pool(name="w_grouped", bufs=2))
        x_grouped_pool = ctx.enter_context(tc.tile_pool(name="x_grouped", bufs=2))
        x_pool = ctx.enter_context(tc.tile_pool(name="x", bufs=EARLY_TILES + 2))
        resid_pool = ctx.enter_context(tc.tile_pool(name="resid", bufs=3))
        u_pool = ctx.enter_context(tc.tile_pool(name="u", bufs=2))
        y_pool = ctx.enter_context(tc.tile_pool(name="y", bufs=3))
        scratch = ctx.enter_context(tc.tile_pool(name="scratch", bufs=2))
        stats = ctx.enter_context(tc.tile_pool(name="stats", bufs=4))
        acc_pool = ctx.enter_context(tc.psum_pool(name="acc", bufs=EARLY_TILES * HALVES))
        stage = ctx.enter_context(tc.psum_pool(name="stage", bufs=STAGE_BANKS))

        ident_words = const.tile([P, P], F32)
        make_identity(nc, ident_words[:])
        ident_bf16 = const.tile([P, P], BF16)
        make_identity(nc, ident_bf16[:])
        vector_rows = const.tile([P, N], BF16)
        nc.vector.memset(vector_rows[:], 0.0)
        pick = const.tile([P, 3, P], BF16)
        nc.vector.memset(pick[:], 0.0)
        for j, vec in enumerate((b_f, ln2_g, ln2_b)):
            nc.sync.dma_start(out=vector_rows[32 * j : 32 * j + 1, :], in_=vec.rearrange("(o n) -> o n", o=1))
            nc.vector.memset(pick[32 * j : 32 * j + 1, j, :], 1.0)
        eps = const.tile([P, 1], F32)
        nc.vector.memset(eps[:], EPS)
        warm = const.tile([P, 1], F32)
        nc.scalar.activation(out=warm[:], in_=eps[:], func=ACT.Sqrt)
        gamma = const.tile([P, N], F32)
        beta = const.tile([P, N], F32)

        def spread_gain_and_shift():
            for h in range(HALVES):
                cols = slice(h * BANK, (h + 1) * BANK)
                gamma_bank = stage.tile([P, BANK], F32, name="bank")
                nc.tensor.matmul(out=gamma_bank[:], lhsT=pick[:, 1, :], rhs=vector_rows[:, cols], start=True, stop=True)
                nc.vector.tensor_copy(out=gamma[:, cols], in_=gamma_bank[:])
                beta_bank = stage.tile([P, BANK], F32, name="bank")
                nc.tensor.matmul(out=beta_bank[:], lhsT=pick[:, 2, :], rhs=vector_rows[:, cols], start=True, stop=True)
                nc.scalar.copy(out=beta[:, cols], in_=beta_bank[:])

        w_codes = const.tile([P, PASSES, N], U32, align_bytes=64)
        w_scales = const.tile([P, PASSES, N], U8, align_bytes=64)

        ff_tile, attn_tile, w_raw, w_grouped = {}, {}, {}, {}
        x_grouped, x_codes, x_scales = {}, {}, {}
        acc, resid, u, y, neg_mean, std = {}, {}, {}, {}, {}, {}

        def load_tokens(m):
            ff_tile[m] = ff_pool.tile([P, K], BF16, name="ff_tile")
            nc.sync.dma_start(out=ff_tile[m][:], in_=ff_rows[m * P : (m + 1) * P, :])

        def load_residual(m):
            attn_tile[m] = attn_pool.tile([P, N], BF16, name="attn_tile")
            nc.sync.dma_start(out=attn_tile[m][:], in_=attn_rows[m * P : (m + 1) * P, :])

        def load_weights(g):
            w_raw[g] = w_raw_pool.tile([P, PACK, N], BF16, name="w_raw")
            nc.sync.dma_start(
                out=w_raw[g][:].rearrange("p (u e) c -> p u (e c)", u=2),
                in_=Wf[g * K_PASS : (g + 1) * K_PASS, :].rearrange("(u p e) c -> p u (e c)", u=2, e=2),
            )

        def regroup_weights(g):
            w_grouped[g] = w_grouped_pool.tile([P, N, PACK], BF16, name="w_grouped", align_bytes=64)
            left = slice(0, W_VECTOR_COLS)
            right = slice(W_VECTOR_COLS, N)
            nc.vector.tensor_copy(
                out=w_grouped[g][:, left, :].rearrange("p (c i) t -> p c t i", i=4),
                in_=w_raw[g][:, :, left].rearrange("p t (c i) -> p c t i", i=4),
            )
            nc.scalar.copy(
                out=w_grouped[g][:, right, :].rearrange("p (c i) t -> p c t i", i=4),
                in_=w_raw[g][:, :, right].rearrange("p t (c i) -> p c t i", i=4),
            )

        def quantise_weights(g):
            for h in range(HALVES):
                cols = slice(h * BANK, (h + 1) * BANK)
                nc.vector.quantize_mx(
                    out=w_codes[:, g, cols].bitcast(FP8X4),
                    scales=w_scales[:, g, cols],
                    in_=w_grouped[g][:, cols, :].rearrange("p c t -> p (c t)"),
                )

        def transpose_tokens(m, j):
            if j == 0:
                x_grouped[m] = x_grouped_pool.tile([P, PASSES * P * PACK], BF16, name="x_grouped", align_bytes=64)
            words = ff_tile[m][:].bitcast(F32)
            bank = stage.tile([P, BANK], F32, name="bank")
            for q in range(BANK // P):
                first = j * BANK + q * P
                nc.tensor.transpose(bank[:, q * P : (q + 1) * P], words[:, first : first + P], ident_words[:])
            nc.scalar.copy(
                out=x_grouped[m][:].bitcast(F32)[:, j * BANK : (j + 1) * BANK].rearrange(
                    "p (g r u) -> p g r u", g=PASSES_PER_FILL, u=2
                ),
                in_=bank[:].rearrange("p (g u r) -> p g r u", g=PASSES_PER_FILL, u=2),
            )

        def quantise_tokens(m):
            x_codes[m] = x_pool.tile([P, PASSES * P], U32, name="x_codes", align_bytes=64)
            x_scales[m] = x_pool.tile([P, PASSES * P], U8, name="x_scales", align_bytes=64)
            width = PASSES_PER_FILL * P
            for j in range(FILLS):
                nc.vector.quantize_mx(
                    out=x_codes[m][:, j * width : (j + 1) * width].bitcast(FP8X4),
                    scales=x_scales[m][:, j * width : (j + 1) * width],
                    in_=x_grouped[m][:, j * width * PACK : (j + 1) * width * PACK],
                )

        def multiply(m, g):
            if g == 0:
                acc[m] = [acc_pool.tile([P, BANK], F32, name="acc") for h in range(HALVES)]
            tokens = slice(g * P, (g + 1) * P)
            for h in range(HALVES):
                cols = slice(h * BANK, (h + 1) * BANK)
                nc.tensor.matmul_mx(
                    out=acc[m][h][:],
                    lhsT=x_codes[m][:, tokens].bitcast(FP8X4),
                    lhsT_scale=x_scales[m][:, tokens],
                    rhs=w_codes[:, g, cols].bitcast(FP8X4),
                    rhs_scale=w_scales[:, g, cols],
                    start=(g == 0),
                    stop=(g == PASSES - 1),
                )

        def add_residual_and_bias(m):
            resid[m] = resid_pool.tile([P, N], F32, name="resid")
            for h in range(HALVES):
                cols = slice(h * BANK, (h + 1) * BANK)
                bank = stage.tile([P, BANK], F32, name="bank")
                nc.tensor.matmul(out=bank[:], lhsT=ident_bf16[:], rhs=attn_tile[m][:, cols], start=True, stop=False)
                nc.tensor.matmul(out=bank[:], lhsT=pick[:, 0, :], rhs=vector_rows[:, cols], start=False, stop=True)
                nc.scalar.copy(out=resid[m][:, cols], in_=bank[:])

        def form_u(m):
            u[m] = u_pool.tile([P, N], F32, name="u")
            half_sums = stats.tile([P, HALVES], F32, name="half_sums")
            for h in range(HALVES):
                cols = slice(h * BANK, (h + 1) * BANK)
                nc.vector.scalar_tensor_tensor(
                    out=u[m][:, cols],
                    in0=acc[m][h][:],
                    scalar=1.0,
                    in1=resid[m][:, cols],
                    op0=ALU.mult,
                    op1=ALU.add,
                    accum_out=half_sums[:, h : h + 1],
                )
            neg_mean[m] = stats.tile([P, 1], F32, name="neg_mean")
            nc.vector.tensor_scalar(
                out=neg_mean[m][:],
                in0=half_sums[:, 0:1],
                scalar1=half_sums[:, 1:2],
                scalar2=-1.0 / N,
                op0=ALU.add,
                op1=ALU.mult,
            )

        def deviation(m):
            squares = scratch.tile([P, N], BF16, name="squares")
            sum_squares = stats.tile([P, 1], F32, name="sum_squares")
            nc.scalar.activation(
                out=squares[:], in_=u[m][:], func=ACT.Square, bias=neg_mean[m][:], scale=1.0, accum_out=sum_squares[:]
            )
            std[m] = stats.tile([P, 1], F32, name="std")
            nc.scalar.activation(out=std[m][:], in_=sum_squares[:], func=ACT.Sqrt, bias=eps[:], scale=1.0 / N)

        def centre_and_gain(m):
            y[m] = y_pool.tile([P, N], F32, name="y")
            nc.vector.scalar_tensor_tensor(
                out=y[m][:], in0=u[m][:], scalar=neg_mean[m][:], in1=gamma[:], op0=ALU.add, op1=ALU.mult
            )

        def scale_shift_store(m):
            rstd = stats.tile([P, 1], F32, name="rstd")
            nc.vector.reciprocal(out=rstd[:], in_=std[m][:])
            nc.vector.scalar_tensor_tensor(
                out=y[m][:], in0=y[m][:], scalar=rstd[:], in1=beta[:], op0=ALU.mult, op1=ALU.add
            )
            nc.sync.dma_start(out=out_rows[m * P : (m + 1) * P, :], in_=y[m][:])

        for step in range(PASSES):
            load_weights(step)
            if step < EARLY_TILES:
                load_tokens(step)
            if step == 0:
                spread_gain_and_shift()
            regroup_weights(step)
            if 1 <= step <= EARLY_TILES:
                quantise_tokens(step - 1)
            quantise_weights(step)
            if step < EARLY_TILES:
                for j in range(FILLS):
                    transpose_tokens(step, j)
            if step == PASSES - 1:
                load_residual(0)
                add_residual_and_bias(0)
            for m in range(EARLY_TILES):
                for g in range(PASSES):
                    if max(m + 1, g) == step:
                        multiply(m, g)

        for m in range(EARLY_TILES, TILES):
            load_tokens(m)
            load_residual(m - EARLY_TILES + 1)
        for m in range(TILES - EARLY_TILES + 1, TILES):
            load_residual(m)
        for j in range(FILLS):
            transpose_tokens(EARLY_TILES, j)

        for s in range(TILES):
            multiplied = s + EARLY_TILES
            transposed = multiplied + 1
            if s + 1 < TILES:
                add_residual_and_bias(s + 1)
            form_u(s)
            deviation(s)
            if s >= 1:
                scale_shift_store(s - 1)
            centre_and_gain(s)
            if multiplied < TILES:
                quantise_tokens(multiplied)
            if transposed < TILES:
                for j in range(FILLS):
                    transpose_tokens(transposed, j)
            if multiplied < TILES:
                for g in range(PASSES):
                    multiply(multiplied, g)
        scale_shift_store(TILES - 1)
